import numpy as np
import ml_dtypes


def mxq(x, axis, fmt="e4m3"):
    dtype, down = {"e4m3": (ml_dtypes.float8_e4m3fn, 7), "e5m2": (ml_dtypes.float8_e5m2, 14)}[fmt]
    v = np.moveaxis(np.asarray(x, np.float32).astype(ml_dtypes.bfloat16).astype(np.float64), axis, -1)
    blocks = v.reshape(v.shape[:-1] + (-1, 32))
    amax = np.abs(blocks).max(-1, keepdims=True)
    byte = np.maximum(np.where(amax > 0, np.frexp(amax)[1] - 1 + 127, 0) - down, 1)
    scale = np.exp2(byte - 127.0)
    codes = (blocks / scale).astype(np.float32).astype(dtype).astype(np.float64)
    return np.moveaxis((codes * scale).reshape(v.shape), -1, axis)


WIDE = False


def mx_kscale(k, group=512):
    if not WIDE:
        return np.ones(k)
    levels = np.array([10, -10, 5, -5, 0])
    if group != 512:
        return np.exp2(np.random.permutation(np.resize(levels, k // group))).repeat(group)
    a = np.random.permutation(np.resize(levels, k // 512 * 4)).reshape(k // 512, 4)
    idx = np.arange(k)
    return np.exp2(a[idx // 512, idx % 128 // 32])


BF16 = ml_dtypes.bfloat16


def bf(x):
    return np.asarray(x, np.float32).astype(BF16)


def f64(x):
    return np.asarray(x).astype(np.float64)


B, IN, OUT = 8192, 1024, 512
QI, QO = IN // 4, OUT // 4


def _hamilton_weight(Wr, Wi, Wj, Wk):
    return np.concatenate([
        np.concatenate([Wr, Wi, Wj, Wk], axis=1),
        np.concatenate([-Wi, Wr, Wk, -Wj], axis=1),
        np.concatenate([-Wj, -Wk, Wr, Wi], axis=1),
        np.concatenate([-Wk, Wj, -Wi, Wr], axis=1),
    ], axis=0)


def _hamilton_bias(br, bi, bj, bk):
    return np.concatenate([
        br - bi - bj - bk,
        br + bi + bj - bk,
        br - bi + bj + bk,
        br + bi - bj + bk,
    ], axis=0)


def setup_inputs():
    s = mx_kscale(QI, group=QI // 4)
    c = 1.0 / np.sqrt(QI)
    return {"x": bf(np.random.standard_normal((B, IN)) * np.tile(s, 4)),
            "Wr": bf(np.random.standard_normal((QI, QO)) * c / s[:, None]),
            "Wi": bf(np.random.standard_normal((QI, QO)) * c / s[:, None]),
            "Wj": bf(np.random.standard_normal((QI, QO)) * c / s[:, None]),
            "Wk": bf(np.random.standard_normal((QI, QO)) * c / s[:, None]),
            "br": bf(np.random.standard_normal(QO) * 0.3),
            "bi": bf(np.random.standard_normal(QO) * 0.3),
            "bj": bf(np.random.standard_normal(QO) * 0.3),
            "bk": bf(np.random.standard_normal(QO) * 0.3)}


def reference(x, Wr, Wi, Wj, Wk, br, bi, bj, bk):
    Wq = mxq(np.concatenate([f64(Wr), f64(Wi), f64(Wj), f64(Wk)], axis=0), 0, "e4m3")
    W = _hamilton_weight(Wq[:QI], Wq[QI:2 * QI], Wq[2 * QI:3 * QI], Wq[3 * QI:])
    b = _hamilton_bias(f64(br), f64(bi), f64(bj), f64(bk))
    return (mxq(f64(x), 1, "e4m3") @ W) + b

@@ -1,0 +1,191 @@
+from contextlib import ExitStack
+
+import concourse.mybir as mybir
+from concourse.masks import make_identity
+
+BF16 = mybir.dt.bfloat16
+F32 = mybir.dt.float32
+U32 = mybir.dt.uint32
+U8 = mybir.dt.uint8
+FP8X4 = mybir.dt.float8_e4m3fn_x4
+
+P = 128
+ROWS, K_IN, N_OUT = 8192, 1024, 512
+COMPONENTS = 4
+QUARTER_OUT = N_OUT // COMPONENTS
+WORDS = K_IN // COMPONENTS // 2
+PASSES = 2
+PACK = 4
+TILES = 4
+GROUP_ROWS = TILES * P
+GROUPS = ROWS // GROUP_ROWS
+X_GROUPS_IN_SBUF = 12
+OUT_GROUPS_IN_SBUF = 10
+
+FLOPS = 2 * ROWS * K_IN * N_OUT
+
+A_BLOCKS = ((("r", 1.0), ("i", 1.0)), (("i", -1.0), ("r", 1.0)))
+B_BLOCKS = ((("j", 1.0), ("k", 1.0)), (("k", 1.0), ("j", -1.0)))
+STRIP = ((B_BLOCKS, -1.0), (A_BLOCKS, 1.0), (B_BLOCKS, 1.0))
+PART_COLS = 2 * QUARTER_OUT
+STRIP_COLS = len(STRIP) * PART_COLS
+
+BIAS_SIGNS = (
+    (1.0, -1.0, -1.0, -1.0),
+    (1.0, 1.0, 1.0, -1.0),
+    (1.0, -1.0, 1.0, 1.0),
+    (1.0, 1.0, -1.0, 1.0),
+)
+QUADRANT = 32
+
+
+def tile_quaternionlinear_t_kernel(tc, x, Wr, Wi, Wj, Wk, br, bi, bj, bk, out):
+    nc = tc.nc
+    with ExitStack() as stack:
+        consts = stack.enter_context(tc.tile_pool(name="consts", bufs=1))
+        x_pool = stack.enter_context(tc.tile_pool(name="x_pool", bufs=X_GROUPS_IN_SBUF))
+        out_pool = stack.enter_context(tc.tile_pool(name="out_pool", bufs=OUT_GROUPS_IN_SBUF))
+        mx_pool = stack.enter_context(tc.tile_pool(name="mx_pool", bufs=2))
+        words_psum = stack.enter_context(tc.psum_pool(name="words_psum", bufs=TILES))
+        acc_psum = stack.enter_context(tc.psum_pool(name="acc_psum", bufs=TILES))
+        stack.enter_context(tc.manual_schedule())
+
+        x_groups = {}
+
+        def load_group(s):
+            x_rows = x_pool.tile([P, TILES, K_IN], BF16, name="x_rows")
+            nc.sync.dma_start(
+                out=x_rows[:],
+                in_=x[s * GROUP_ROWS : (s + 1) * GROUP_ROWS, :].rearrange(
+                    "(p t) k -> p t k", t=TILES
+                ),
+            )
+            x_groups[s] = x_rows
+
+        w_raw = {}
+        for name, w in (("r", Wr), ("i", Wi), ("j", Wj), ("k", Wk)):
+            w_raw[name] = consts.tile([P, 2, QUARTER_OUT], BF16, name="w_raw_" + name)
+            nc.scalar.dma_start(out=w_raw[name][:], in_=w.rearrange("(p e) n -> p e n", e=2))
+        for s in range(X_GROUPS_IN_SBUF):
+            load_group(s)
+
+        identity = consts.tile([P, P], F32, name="identity")
+        make_identity(nc, identity[:])
+
+        bias_rows = consts.tile([P, QUARTER_OUT], BF16, name="bias_rows")
+        nc.vector.memset(bias_rows[:], 0.0)
+        for m, b in enumerate((br, bi, bj, bk)):
+            nc.gpsimd.dma_start(
+                out=bias_rows[m * QUADRANT : m * QUADRANT + 1, :],
+                in_=b.rearrange("(o n) -> o n", o=1),
+            )
+        bias_signs = consts.tile([P, COMPONENTS, P], BF16, name="bias_signs")
+        nc.vector.memset(bias_signs[:], 1.0)
+        for o in range(COMPONENTS):
+            for m in range(COMPONENTS):
+                if BIAS_SIGNS[o][m] < 0.0:
+                    nc.vector.memset(bias_signs[m * QUADRANT : (m + 1) * QUADRANT, o, :], -1.0)
+
+        w_grouped = consts.tile([P, STRIP_COLS, PACK], BF16, name="w_grouped", align_bytes=64)
+        w_codes = consts.tile([P, STRIP_COLS], U32, name="w_codes", align_bytes=64)
+        w_scales = consts.tile([P, STRIP_COLS], U8, name="w_scales", align_bytes=64)
+        for part, (blocks, part_sign) in enumerate(STRIP):
+            for u in range(2):
+                for half in range(2):
+                    name, sign = blocks[u][half]
+                    first_col = part * PART_COLS + half * QUARTER_OUT
+                    dst = w_grouped[:, first_col : first_col + QUARTER_OUT, 2 * u : 2 * u + 2]
+                    src = w_raw[name][:].rearrange("p e n -> p n e")
+                    if part == 0:
+                        nc.scalar.mul(out=dst, in_=src, mul=sign * part_sign)
+                    else:
+                        nc.vector.tensor_scalar_mul(out=dst, in0=src, scalar1=sign * part_sign)
+        for part in range(len(STRIP)):
+            cols = slice(part * PART_COLS, (part + 1) * PART_COLS)
+            nc.vector.quantize_mx(
+                out=w_codes[:, cols].bitcast(FP8X4),
+                scales=w_scales[:, cols],
+                in_=w_grouped[:, cols, :].rearrange("p n t -> p (n t)"),
+            )
+
+        x_grouped = {}
+        x_codes = {}
+        x_scales = {}
+
+        def transpose_group(s):
+            x_grouped[s] = mx_pool.tile(
+                [P, TILES * PASSES * P * PACK], BF16, name="x_grouped", align_bytes=64
+            )
+            grouped_words = (
+                x_grouped[s][:]
+                .bitcast(F32)
+                .rearrange("p (t g r u) -> p t g r u", t=TILES, g=PASSES, r=P)
+            )
+            for t in range(TILES):
+                x_words = x_groups[s][:, t, :].bitcast(F32)
+                flipped = words_psum.tile([P, COMPONENTS, P], F32, name="flipped")
+                for c in range(COMPONENTS):
+                    nc.tensor.transpose(
+                        out=flipped[:, c, :],
+                        in_=x_words[:, c * WORDS : (c + 1) * WORDS],
+                        identity=identity[:],
+                    )
+                nc.scalar.copy(
+                    out=grouped_words[:, t, :, :, :],
+                    in_=flipped[:].rearrange("p (g u) r -> p g r u", u=2),
+                )
+
+        def quantise_group(s):
+            x_codes[s] = mx_pool.tile([P, TILES, PASSES, P], U32, name="x_codes", align_bytes=64)
+            x_scales[s] = mx_pool.tile([P, TILES, PASSES, P], U8, name="x_scales", align_bytes=64)
+            nc.vector.quantize_mx(
+                out=x_codes[s][:].rearrange("p t g r -> p (t g r)").bitcast(FP8X4),
+                scales=x_scales[s][:].rearrange("p t g r -> p (t g r)"),
+                in_=x_grouped[s][:],
+            )
+
+        def multiply_group(s):
+            out_rows = out_pool.tile([P, TILES, N_OUT], F32, name="out_rows")
+            for t in range(TILES):
+                acc = acc_psum.tile([P, N_OUT], F32, name="acc", tag="acc")
+                for g in range(PASSES):
+                    strip_cols = slice((1 - g) * PART_COLS, (1 - g) * PART_COLS + N_OUT)
+                    nc.tensor.matmul_mx(
+                        out=acc[:],
+                        lhsT=x_codes[s][:, t, g, :].bitcast(FP8X4),
+                        lhsT_scale=x_scales[s][:, t, g, :],
+                        rhs=w_codes[:, strip_cols].bitcast(FP8X4),
+                        rhs_scale=w_scales[:, strip_cols],
+                        start=(g == 0),
+                        stop=(g == PASSES - 1),
+                    )
+                nc.vector.tensor_add(out=out_rows[:, t, :], in0=acc[:], in1=bias[:])
+            nc.sync.dma_start(
+                out=out[s * GROUP_ROWS : (s + 1) * GROUP_ROWS, :].rearrange(
+                    "(p t) n -> p t n", t=TILES
+                ),
+                in_=out_rows[:],
+            )
+
+        transpose_group(0)
+        quantise_group(0)
+
+        bias_psum = acc_psum.tile([P, N_OUT], F32, name="bias_psum", tag="acc")
+        for o in range(COMPONENTS):
+            nc.tensor.matmul(
+                out=bias_psum[:, o * QUARTER_OUT : (o + 1) * QUARTER_OUT],
+                lhsT=bias_signs[:, o, :],
+                rhs=bias_rows[:],
+                start=True,
+                stop=True,
+            )
+        bias = consts.tile([P, N_OUT], F32, name="bias")
+        nc.vector.tensor_copy(out=bias[:], in_=bias_psum[:])
+
+        for s in range(GROUPS):
+            if s + X_GROUPS_IN_SBUF < GROUPS:
+                load_group(s + X_GROUPS_IN_SBUF)
+            if s + 1 < GROUPS:
+                transpose_group(s + 1)
+                quantise_group(s + 1)
+            multiply_group(s)

@@ -21,6 +21,9 @@ GROUP_ROWS = TILES * P
 GROUPS = ROWS // GROUP_ROWS
 X_GROUPS_IN_SBUF = 12
 OUT_GROUPS_IN_SBUF = 10
+FIRST_LOAD_PIECES = 2
+LAST_STORE_PIECES = TILES
+EARLY_GROUPS = 3
 
 FLOPS = 2 * ROWS * K_IN * N_OUT
 
@@ -54,31 +57,33 @@ def tile_quaternionlinear_t_kernel(tc, x, Wr, Wi, Wj, Wk, br, bi, bj, bk, out):
 
         def load_group(s):
             x_rows = x_pool.tile([P, TILES, K_IN], BF16, name="x_rows")
-            nc.sync.dma_start(
-                out=x_rows[:],
-                in_=x[s * GROUP_ROWS : (s + 1) * GROUP_ROWS, :].rearrange(
-                    "(p t) k -> p t k", t=TILES
-                ),
+            x_view = x[s * GROUP_ROWS : (s + 1) * GROUP_ROWS, :].rearrange(
+                "(p t) k -> p t k", t=TILES
             )
+            piece = TILES // (FIRST_LOAD_PIECES if s == 0 else 1)
+            for t in range(0, TILES, piece):
+                nc.sync.dma_start(out=x_rows[:, t : t + piece, :], in_=x_view[:, t : t + piece, :])
             x_groups[s] = x_rows
 
         w_raw = {}
         for name, w in (("r", Wr), ("i", Wi), ("j", Wj), ("k", Wk)):
             w_raw[name] = consts.tile([P, 2, QUARTER_OUT], BF16, name="w_raw_" + name)
             nc.scalar.dma_start(out=w_raw[name][:], in_=w.rearrange("(p e) n -> p e n", e=2))
-        for s in range(X_GROUPS_IN_SBUF):
+        for s in range(EARLY_GROUPS):
+            load_group(s)
+        bias_rows = consts.tile([P, QUARTER_OUT], BF16, name="bias_rows")
+        nc.vector.memset(bias_rows[:], 0.0)
+        for m, b in enumerate((br, bi, bj, bk)):
+            nc.sync.dma_start(
+                out=bias_rows[m * QUADRANT : m * QUADRANT + 1, :],
+                in_=b.rearrange("(o n) -> o n", o=1),
+            )
+        for s in range(EARLY_GROUPS, X_GROUPS_IN_SBUF):
             load_group(s)
 
         identity = consts.tile([P, P], F32, name="identity")
         make_identity(nc, identity[:])
 
-        bias_rows = consts.tile([P, QUARTER_OUT], BF16, name="bias_rows")
-        nc.vector.memset(bias_rows[:], 0.0)
-        for m, b in enumerate((br, bi, bj, bk)):
-            nc.gpsimd.dma_start(
-                out=bias_rows[m * QUADRANT : m * QUADRANT + 1, :],
-                in_=b.rearrange("(o n) -> o n", o=1),
-            )
         bias_signs = consts.tile([P, COMPONENTS, P], BF16, name="bias_signs")
         nc.vector.memset(bias_signs[:], 1.0)
         for o in range(COMPONENTS):
@@ -146,6 +151,10 @@ def tile_quaternionlinear_t_kernel(tc, x, Wr, Wi, Wj, Wk, br, bi, bj, bk, out):
 
         def multiply_group(s):
             out_rows = out_pool.tile([P, TILES, N_OUT], F32, name="out_rows")
+            out_view = out[s * GROUP_ROWS : (s + 1) * GROUP_ROWS, :].rearrange(
+                "(p t) n -> p t n", t=TILES
+            )
+            piece = TILES // (LAST_STORE_PIECES if s == GROUPS - 1 else 1)
             for t in range(TILES):
                 acc = acc_psum.tile([P, N_OUT], F32, name="acc", tag="acc")
                 for g in range(PASSES):
@@ -160,15 +169,13 @@ def tile_quaternionlinear_t_kernel(tc, x, Wr, Wi, Wj, Wk, br, bi, bj, bk, out):
                         stop=(g == PASSES - 1),
                     )
                 nc.vector.tensor_add(out=out_rows[:, t, :], in0=acc[:], in1=bias[:])
-            nc.sync.dma_start(
-                out=out[s * GROUP_ROWS : (s + 1) * GROUP_ROWS, :].rearrange(
-                    "(p t) n -> p t n", t=TILES
-                ),
-                in_=out_rows[:],
-            )
+                if (t + 1) % piece == 0:
+                    done = slice(t + 1 - piece, t + 1)
+                    nc.sync.dma_start(out=out_view[:, done, :], in_=out_rows[:, done, :])
 
-        transpose_group(0)
-        quantise_group(0)
+        for s in range(2):
+            transpose_group(s)
+            quantise_group(s)
 
         bias_psum = acc_psum.tile([P, N_OUT], F32, name="bias_psum", tag="acc")
         for o in range(COMPONENTS):
@@ -185,7 +192,7 @@ def tile_quaternionlinear_t_kernel(tc, x, Wr, Wi, Wj, Wk, br, bi, bj, bk, out):
         for s in range(GROUPS):
             if s + X_GROUPS_IN_SBUF < GROUPS:
                 load_group(s + X_GROUPS_IN_SBUF)
-            if s + 1 < GROUPS:
-                transpose_group(s + 1)
-                quantise_group(s + 1)
             multiply_group(s)
+            if s + 2 < GROUPS:
+                transpose_group(s + 2)
+                quantise_group(s + 2)

@@ -17,13 +17,14 @@ WORDS = K_IN // COMPONENTS // 2
 PASSES = 2
 PACK = 4
 TILES = 4
-GROUP_ROWS = TILES * P
-GROUPS = ROWS // GROUP_ROWS
-X_GROUPS_IN_SBUF = 12
-OUT_GROUPS_IN_SBUF = 10
-FIRST_LOAD_PIECES = 2
-LAST_STORE_PIECES = TILES
-EARLY_GROUPS = 3
+GROUPS = ROWS // (TILES * P)
+BLOCK_GROUPS = 2
+BLOCK_TILES = BLOCK_GROUPS * TILES
+BLOCK_ROWS = BLOCK_TILES * P
+BLOCKS = ROWS // BLOCK_ROWS
+X_BLOCKS_IN_SBUF = 6
+OUT_BLOCKS_IN_SBUF = 5
+EDGE_TILES = 2
 
 FLOPS = 2 * ROWS * K_IN * N_OUT
 
@@ -46,40 +47,41 @@ def tile_quaternionlinear_t_kernel(tc, x, Wr, Wi, Wj, Wk, br, bi, bj, bk, out):
     nc = tc.nc
     with ExitStack() as stack:
         consts = stack.enter_context(tc.tile_pool(name="consts", bufs=1))
-        x_pool = stack.enter_context(tc.tile_pool(name="x_pool", bufs=X_GROUPS_IN_SBUF))
-        out_pool = stack.enter_context(tc.tile_pool(name="out_pool", bufs=OUT_GROUPS_IN_SBUF))
+        x_pool = stack.enter_context(tc.tile_pool(name="x_pool", bufs=X_BLOCKS_IN_SBUF))
+        out_pool = stack.enter_context(tc.tile_pool(name="out_pool", bufs=OUT_BLOCKS_IN_SBUF))
         mx_pool = stack.enter_context(tc.tile_pool(name="mx_pool", bufs=2))
         words_psum = stack.enter_context(tc.psum_pool(name="words_psum", bufs=TILES))
         acc_psum = stack.enter_context(tc.psum_pool(name="acc_psum", bufs=TILES))
         stack.enter_context(tc.manual_schedule())
 
-        x_groups = {}
+        x_blocks = {}
+        out_blocks = {}
 
-        def load_group(s):
-            x_rows = x_pool.tile([P, TILES, K_IN], BF16, name="x_rows")
-            x_view = x[s * GROUP_ROWS : (s + 1) * GROUP_ROWS, :].rearrange(
-                "(p t) k -> p t k", t=TILES
+        def load_block(b):
+            x_blocks[b] = x_pool.tile([P, BLOCK_TILES, K_IN], BF16, name="x_block")
+            x_view = x[b * BLOCK_ROWS : (b + 1) * BLOCK_ROWS, :].rearrange(
+                "(p j) k -> p j k", j=BLOCK_TILES
             )
-            piece = TILES // (FIRST_LOAD_PIECES if s == 0 else 1)
-            for t in range(0, TILES, piece):
-                nc.sync.dma_start(out=x_rows[:, t : t + piece, :], in_=x_view[:, t : t + piece, :])
-            x_groups[s] = x_rows
+            piece = EDGE_TILES if b == 0 else BLOCK_TILES
+            for j in range(0, BLOCK_TILES, piece):
+                nc.sync.dma_start(
+                    out=x_blocks[b][:, j : j + piece, :], in_=x_view[:, j : j + piece, :]
+                )
 
         w_raw = {}
         for name, w in (("r", Wr), ("i", Wi), ("j", Wj), ("k", Wk)):
             w_raw[name] = consts.tile([P, 2, QUARTER_OUT], BF16, name="w_raw_" + name)
             nc.scalar.dma_start(out=w_raw[name][:], in_=w.rearrange("(p e) n -> p e n", e=2))
-        for s in range(EARLY_GROUPS):
-            load_group(s)
+        load_block(0)
         bias_rows = consts.tile([P, QUARTER_OUT], BF16, name="bias_rows")
         nc.vector.memset(bias_rows[:], 0.0)
-        for m, b in enumerate((br, bi, bj, bk)):
+        for m, bias_vector in enumerate((br, bi, bj, bk)):
             nc.sync.dma_start(
                 out=bias_rows[m * QUADRANT : m * QUADRANT + 1, :],
-                in_=b.rearrange("(o n) -> o n", o=1),
+                in_=bias_vector.rearrange("(o n) -> o n", o=1),
             )
-        for s in range(EARLY_GROUPS, X_GROUPS_IN_SBUF):
-            load_group(s)
+        for b in range(1, X_BLOCKS_IN_SBUF):
+            load_block(b)
 
         identity = consts.tile([P, P], F32, name="identity")
         make_identity(nc, identity[:])
@@ -118,6 +120,7 @@ def tile_quaternionlinear_t_kernel(tc, x, Wr, Wi, Wj, Wk, br, bi, bj, bk, out):
         x_scales = {}
 
         def transpose_group(s):
+            b, first_tile = s // BLOCK_GROUPS, (s % BLOCK_GROUPS) * TILES
             x_grouped[s] = mx_pool.tile(
                 [P, TILES * PASSES * P * PACK], BF16, name="x_grouped", align_bytes=64
             )
@@ -127,7 +130,7 @@ def tile_quaternionlinear_t_kernel(tc, x, Wr, Wi, Wj, Wk, br, bi, bj, bk, out):
                 .rearrange("p (t g r u) -> p t g r u", t=TILES, g=PASSES, r=P)
             )
             for t in range(TILES):
-                x_words = x_groups[s][:, t, :].bitcast(F32)
+                x_words = x_blocks[b][:, first_tile + t, :].bitcast(F32)
                 flipped = words_psum.tile([P, COMPONENTS, P], F32, name="flipped")
                 for c in range(COMPONENTS):
                     nc.tensor.transpose(
@@ -139,6 +142,8 @@ def tile_quaternionlinear_t_kernel(tc, x, Wr, Wi, Wj, Wk, br, bi, bj, bk, out):
                     out=grouped_words[:, t, :, :, :],
                     in_=flipped[:].rearrange("p (g u) r -> p g r u", u=2),
                 )
+            if first_tile + TILES == BLOCK_TILES and b + X_BLOCKS_IN_SBUF < BLOCKS:
+                load_block(b + X_BLOCKS_IN_SBUF)
 
         def quantise_group(s):
             x_codes[s] = mx_pool.tile([P, TILES, PASSES, P], U32, name="x_codes", align_bytes=64)
@@ -150,12 +155,15 @@ def tile_quaternionlinear_t_kernel(tc, x, Wr, Wi, Wj, Wk, br, bi, bj, bk, out):
             )
 
         def multiply_group(s):
-            out_rows = out_pool.tile([P, TILES, N_OUT], F32, name="out_rows")
-            out_view = out[s * GROUP_ROWS : (s + 1) * GROUP_ROWS, :].rearrange(
-                "(p t) n -> p t n", t=TILES
+            b, first_tile = s // BLOCK_GROUPS, (s % BLOCK_GROUPS) * TILES
+            if first_tile == 0:
+                out_blocks[b] = out_pool.tile([P, BLOCK_TILES, N_OUT], F32, name="out_block")
+            out_view = out[b * BLOCK_ROWS : (b + 1) * BLOCK_ROWS, :].rearrange(
+                "(p j) n -> p j n", j=BLOCK_TILES
             )
-            piece = TILES // (LAST_STORE_PIECES if s == GROUPS - 1 else 1)
+            piece = EDGE_TILES if b == BLOCKS - 1 else BLOCK_TILES
             for t in range(TILES):
+                j = first_tile + t
                 acc = acc_psum.tile([P, N_OUT], F32, name="acc", tag="acc")
                 for g in range(PASSES):
                     strip_cols = slice((1 - g) * PART_COLS, (1 - g) * PART_COLS + N_OUT)
@@ -168,10 +176,16 @@ def tile_quaternionlinear_t_kernel(tc, x, Wr, Wi, Wj, Wk, br, bi, bj, bk, out):
                         start=(g == 0),
                         stop=(g == PASSES - 1),
                     )
-                nc.vector.tensor_add(out=out_rows[:, t, :], in0=acc[:], in1=bias[:])
-                if (t + 1) % piece == 0:
-                    done = slice(t + 1 - piece, t + 1)
-                    nc.sync.dma_start(out=out_view[:, done, :], in_=out_rows[:, done, :])
+                if t == TILES - 1 and s + 2 < GROUPS:
+                    nc.scalar.copy(out=out_blocks[b][:, j, :], in_=acc[:])
+                    nc.gpsimd.tensor_add(
+                        out=out_blocks[b][:, j, :], in0=out_blocks[b][:, j, :], in1=bias[:]
+                    )
+                else:
+                    nc.vector.tensor_add(out=out_blocks[b][:, j, :], in0=acc[:], in1=bias[:])
+                if (j + 1) % piece == 0:
+                    done = slice(j + 1 - piece, j + 1)
+                    nc.sync.dma_start(out=out_view[:, done, :], in_=out_blocks[b][:, done, :])
 
         for s in range(2):
             transpose_group(s)
@@ -190,8 +204,6 @@ def tile_quaternionlinear_t_kernel(tc, x, Wr, Wi, Wj, Wk, br, bi, bj, bk, out):
         nc.vector.tensor_copy(out=bias[:], in_=bias_psum[:])
 
         for s in range(GROUPS):
-            if s + X_GROUPS_IN_SBUF < GROUPS:
-                load_group(s + X_GROUPS_IN_SBUF)
             multiply_group(s)
             if s + 2 < GROUPS:
                 transpose_group(s + 2)

@@ -22,8 +22,8 @@ BLOCK_GROUPS = 2
 BLOCK_TILES = BLOCK_GROUPS * TILES
 BLOCK_ROWS = BLOCK_TILES * P
 BLOCKS = ROWS // BLOCK_ROWS
-X_BLOCKS_IN_SBUF = 6
-OUT_BLOCKS_IN_SBUF = 5
+X_BLOCKS_IN_SBUF = 8
+OUT_BLOCKS_IN_SBUF = 4
 EDGE_TILES = 2
 
 FLOPS = 2 * ROWS * K_IN * N_OUT

@@ -176,13 +176,7 @@ def tile_quaternionlinear_t_kernel(tc, x, Wr, Wi, Wj, Wk, br, bi, bj, bk, out):
                         start=(g == 0),
                         stop=(g == PASSES - 1),
                     )
-                if t == TILES - 1 and s + 2 < GROUPS:
-                    nc.scalar.copy(out=out_blocks[b][:, j, :], in_=acc[:])
-                    nc.gpsimd.tensor_add(
-                        out=out_blocks[b][:, j, :], in0=out_blocks[b][:, j, :], in1=bias[:]
-                    )
-                else:
-                    nc.vector.tensor_add(out=out_blocks[b][:, j, :], in0=acc[:], in1=bias[:])
+                nc.vector.tensor_add(out=out_blocks[b][:, j, :], in0=acc[:], in1=bias[:])
                 if (j + 1) % piece == 0:
                     done = slice(j + 1 - piece, j + 1)
                     nc.sync.dma_start(out=out_view[:, done, :], in_=out_blocks[b][:, done, :])

@@ -28,9 +28,12 @@ EDGE_TILES = 2
 
 FLOPS = 2 * ROWS * K_IN * N_OUT
 
-A_BLOCKS = ((("r", 1.0), ("i", 1.0)), (("i", -1.0), ("r", 1.0)))
-B_BLOCKS = ((("j", 1.0), ("k", 1.0)), (("k", 1.0), ("j", -1.0)))
-STRIP = ((B_BLOCKS, -1.0), (A_BLOCKS, 1.0), (B_BLOCKS, 1.0))
+SLOTS = ("+i", "+r", "-i", "-k", "+j", "+k", "-j", "-k again")
+STRIP = (
+    (("-j", "-k again"), ("-k", "+j")),
+    (("+r", "-i"), ("+i", "+r")),
+    (("+j", "+k"), ("+k", "-j")),
+)
 PART_COLS = 2 * QUARTER_OUT
 STRIP_COLS = len(STRIP) * PART_COLS
 
@@ -68,10 +71,11 @@ def tile_quaternionlinear_t_kernel(tc, x, Wr, Wi, Wj, Wk, br, bi, bj, bk, out):
                     out=x_blocks[b][:, j : j + piece, :], in_=x_view[:, j : j + piece, :]
                 )
 
-        w_raw = {}
-        for name, w in (("r", Wr), ("i", Wi), ("j", Wj), ("k", Wk)):
-            w_raw[name] = consts.tile([P, 2, QUARTER_OUT], BF16, name="w_raw_" + name)
-            nc.scalar.dma_start(out=w_raw[name][:], in_=w.rearrange("(p e) n -> p e n", e=2))
+        w_slots = consts.tile([P, len(SLOTS), 2, QUARTER_OUT], BF16, name="w_slots")
+        for slot, w in ((0, Wi), (1, Wr), (4, Wj), (5, Wk)):
+            nc.scalar.dma_start(
+                out=w_slots[:, slot, :, :], in_=w.rearrange("(p e) n -> p e n", e=2)
+            )
         load_block(0)
         bias_rows = consts.tile([P, QUARTER_OUT], BF16, name="bias_rows")
         nc.vector.memset(bias_rows[:], 0.0)
@@ -96,19 +100,25 @@ def tile_quaternionlinear_t_kernel(tc, x, Wr, Wi, Wj, Wk, br, bi, bj, bk, out):
         w_grouped = consts.tile([P, STRIP_COLS, PACK], BF16, name="w_grouped", align_bytes=64)
         w_codes = consts.tile([P, STRIP_COLS], U32, name="w_codes", align_bytes=64)
         w_scales = consts.tile([P, STRIP_COLS], U8, name="w_scales", align_bytes=64)
-        for part, (blocks, part_sign) in enumerate(STRIP):
-            for u in range(2):
-                for half in range(2):
-                    name, sign = blocks[u][half]
-                    first_col = part * PART_COLS + half * QUARTER_OUT
-                    dst = w_grouped[:, first_col : first_col + QUARTER_OUT, 2 * u : 2 * u + 2]
-                    src = w_raw[name][:].rearrange("p e n -> p n e")
-                    if part == 0:
-                        nc.scalar.mul(out=dst, in_=src, mul=sign * part_sign)
-                    else:
-                        nc.vector.tensor_scalar_mul(out=dst, in0=src, scalar1=sign * part_sign)
-        for part in range(len(STRIP)):
-            cols = slice(part * PART_COLS, (part + 1) * PART_COLS)
+        nc.vector.tensor_scalar_mul(
+            out=w_slots[:, 2:4, :, :], in0=w_slots[:, 0:6:5, :, :], scalar1=-1.0
+        )
+        nc.vector.tensor_scalar_mul(
+            out=w_slots[:, 6:8, :, :], in0=w_slots[:, 4:6, :, :], scalar1=-1.0
+        )
+        for part, half in ((1, 0), (1, 1), (2, 0), (2, 1), (0, 0), (0, 1)):
+            upper, lower = STRIP[part][half]
+            slot = SLOTS.index(upper)
+            assert SLOTS[slot + 1] == lower
+            first_col = part * PART_COLS + half * QUARTER_OUT
+            copy = nc.scalar.copy if part == 0 else nc.vector.tensor_copy
+            copy(
+                out=w_grouped[:, first_col : first_col + QUARTER_OUT, :].rearrange(
+                    "p n (u e) -> p n u e", u=2
+                ),
+                in_=w_slots[:, slot : slot + 2, :, :].rearrange("p u e n -> p n u e"),
+            )
+        for cols in (slice(PART_COLS, STRIP_COLS), slice(0, PART_COLS)):
             nc.vector.quantize_mx(
                 out=w_codes[:, cols].bitcast(FP8X4),
                 scales=w_scales[:, cols],

@@ -73,7 +73,7 @@ def tile_quaternionlinear_t_kernel(tc, x, Wr, Wi, Wj, Wk, br, bi, bj, bk, out):
 
         w_slots = consts.tile([P, len(SLOTS), 2, QUARTER_OUT], BF16, name="w_slots")
         for slot, w in ((0, Wi), (1, Wr), (4, Wj), (5, Wk)):
-            nc.scalar.dma_start(
+            nc.sync.dma_start(
                 out=w_slots[:, slot, :, :], in_=w.rearrange("(p e) n -> p e n", e=2)
             )
         load_block(0)

@@ -205,7 +205,7 @@ def tile_quaternionlinear_t_kernel(tc, x, Wr, Wi, Wj, Wk, br, bi, bj, bk, out):
                 stop=True,
             )
         bias = consts.tile([P, N_OUT], F32, name="bias")
-        nc.vector.tensor_copy(out=bias[:], in_=bias_psum[:])
+        nc.scalar.copy(out=bias[:], in_=bias_psum[:])
 
         for s in range(GROUPS):
             multiply_group(s)

@@ -24,6 +24,7 @@ BLOCK_ROWS = BLOCK_TILES * P
 BLOCKS = ROWS // BLOCK_ROWS
 X_BLOCKS_IN_SBUF = 8
 OUT_BLOCKS_IN_SBUF = 4
+TRANSPOSED_AHEAD = 3
 EDGE_TILES = 2
 
 FLOPS = 2 * ROWS * K_IN * N_OUT
@@ -152,8 +153,6 @@ def tile_quaternionlinear_t_kernel(tc, x, Wr, Wi, Wj, Wk, br, bi, bj, bk, out):
                     out=grouped_words[:, t, :, :, :],
                     in_=flipped[:].rearrange("p (g u) r -> p g r u", u=2),
                 )
-            if first_tile + TILES == BLOCK_TILES and b + X_BLOCKS_IN_SBUF < BLOCKS:
-                load_block(b + X_BLOCKS_IN_SBUF)
 
         def quantise_group(s):
             x_codes[s] = mx_pool.tile([P, TILES, PASSES, P], U32, name="x_codes", align_bytes=64)
@@ -207,8 +206,11 @@ def tile_quaternionlinear_t_kernel(tc, x, Wr, Wi, Wj, Wk, br, bi, bj, bk, out):
         bias = consts.tile([P, N_OUT], F32, name="bias")
         nc.scalar.copy(out=bias[:], in_=bias_psum[:])
 
+        transposed = 2
         for s in range(GROUPS):
             multiply_group(s)
+            while transposed < min(s + 1 + TRANSPOSED_AHEAD, GROUPS):
+                transpose_group(transposed)
+                transposed += 1
             if s + 2 < GROUPS:
-                transpose_group(s + 2)
                 quantise_group(s + 2)

@@ -15,17 +15,16 @@ COMPONENTS = 4
 QUARTER_OUT = N_OUT // COMPONENTS
 WORDS = K_IN // COMPONENTS // 2
 PASSES = 2
+TILES_OF_A_QUANTIZE = 4
 PACK = 4
-TILES = 4
-GROUPS = ROWS // (TILES * P)
-BLOCK_GROUPS = 2
-BLOCK_TILES = BLOCK_GROUPS * TILES
-BLOCK_ROWS = BLOCK_TILES * P
-BLOCKS = ROWS // BLOCK_ROWS
-X_BLOCKS_IN_SBUF = 8
-OUT_BLOCKS_IN_SBUF = 4
+ROW_TILES = ROWS // P
+LOADS = (2, 2, 4, 4, 4, 4, 4, 8, 8, 8, 8, 8)
+LOADS_BEFORE_BIAS = 2
+STORES = (8,) * 7 + (2,) * 4
+GROUPS = (2, 2, 2, 2, 4, 4) + (6,) * 8
+FIRST_TILE = [sum(GROUPS[:s]) for s in range(len(GROUPS))]
+WORDS_BANKS, ACC_BANKS = 5, 3
 TRANSPOSED_AHEAD = 3
-EDGE_TILES = 2
 
 FLOPS = 2 * ROWS * K_IN * N_OUT
 
@@ -51,33 +50,31 @@ def tile_quaternionlinear_t_kernel(tc, x, Wr, Wi, Wj, Wk, br, bi, bj, bk, out):
     nc = tc.nc
     with ExitStack() as stack:
         consts = stack.enter_context(tc.tile_pool(name="consts", bufs=1))
-        x_pool = stack.enter_context(tc.tile_pool(name="x_pool", bufs=X_BLOCKS_IN_SBUF))
-        out_pool = stack.enter_context(tc.tile_pool(name="out_pool", bufs=OUT_BLOCKS_IN_SBUF))
+        rows_pool = stack.enter_context(tc.tile_pool(name="rows_pool", bufs=1))
         mx_pool = stack.enter_context(tc.tile_pool(name="mx_pool", bufs=2))
-        words_psum = stack.enter_context(tc.psum_pool(name="words_psum", bufs=TILES))
-        acc_psum = stack.enter_context(tc.psum_pool(name="acc_psum", bufs=TILES))
+        words_psum = stack.enter_context(tc.psum_pool(name="words_psum", bufs=WORDS_BANKS))
+        acc_psum = stack.enter_context(tc.psum_pool(name="acc_psum", bufs=ACC_BANKS))
         stack.enter_context(tc.manual_schedule())
 
-        x_blocks = {}
-        out_blocks = {}
+        rows = rows_pool.tile([P, ROW_TILES, N_OUT], F32, name="rows", align_bytes=64)
+        x_view = x.rearrange("(p j) k -> p j k", j=ROW_TILES)
+        out_view = out.rearrange("(p j) n -> p j n", j=ROW_TILES)
 
-        def load_block(b):
-            x_blocks[b] = x_pool.tile([P, BLOCK_TILES, K_IN], BF16, name="x_block")
-            x_view = x[b * BLOCK_ROWS : (b + 1) * BLOCK_ROWS, :].rearrange(
-                "(p j) k -> p j k", j=BLOCK_TILES
+        def load_rows(first, tiles):
+            nc.sync.dma_start(
+                out=rows[:, first : first + tiles, :].bitcast(BF16),
+                in_=x_view[:, first : first + tiles, :],
             )
-            piece = EDGE_TILES if b == 0 else BLOCK_TILES
-            for j in range(0, BLOCK_TILES, piece):
-                nc.sync.dma_start(
-                    out=x_blocks[b][:, j : j + piece, :], in_=x_view[:, j : j + piece, :]
-                )
+
+        x_loads = [(n, sum(LOADS[:i])) for i, n in enumerate(LOADS)]
 
         w_slots = consts.tile([P, len(SLOTS), 2, QUARTER_OUT], BF16, name="w_slots")
         for slot, w in ((0, Wi), (1, Wr), (4, Wj), (5, Wk)):
             nc.sync.dma_start(
                 out=w_slots[:, slot, :, :], in_=w.rearrange("(p e) n -> p e n", e=2)
             )
-        load_block(0)
+        for tiles, first in x_loads[:LOADS_BEFORE_BIAS]:
+            load_rows(first, tiles)
         bias_rows = consts.tile([P, QUARTER_OUT], BF16, name="bias_rows")
         nc.vector.memset(bias_rows[:], 0.0)
         for m, bias_vector in enumerate((br, bi, bj, bk)):
@@ -85,8 +82,8 @@ def tile_quaternionlinear_t_kernel(tc, x, Wr, Wi, Wj, Wk, br, bi, bj, bk, out):
                 out=bias_rows[m * QUADRANT : m * QUADRANT + 1, :],
                 in_=bias_vector.rearrange("(o n) -> o n", o=1),
             )
-        for b in range(1, X_BLOCKS_IN_SBUF):
-            load_block(b)
+        for tiles, first in x_loads[LOADS_BEFORE_BIAS:]:
+            load_rows(first, tiles)
 
         identity = consts.tile([P, P], F32, name="identity")
         make_identity(nc, identity[:])
@@ -129,24 +126,24 @@ def tile_quaternionlinear_t_kernel(tc, x, Wr, Wi, Wj, Wk, br, bi, bj, bk, out):
         x_grouped = {}
         x_codes = {}
         x_scales = {}
+        accs = {}
 
         def transpose_group(s):
-            b, first_tile = s // BLOCK_GROUPS, (s % BLOCK_GROUPS) * TILES
+            tiles = GROUPS[s]
             x_grouped[s] = mx_pool.tile(
-                [P, TILES * PASSES * P * PACK], BF16, name="x_grouped", align_bytes=64
+                [P, tiles * PASSES * P * PACK], BF16, name="x_grouped", align_bytes=64
             )
             grouped_words = (
                 x_grouped[s][:]
                 .bitcast(F32)
-                .rearrange("p (t g r u) -> p t g r u", t=TILES, g=PASSES, r=P)
+                .rearrange("p (t g r u) -> p t g r u", t=tiles, g=PASSES, r=P)
             )
-            for t in range(TILES):
-                x_words = x_blocks[b][:, first_tile + t, :].bitcast(F32)
-                flipped = words_psum.tile([P, COMPONENTS, P], F32, name="flipped")
+            for t in range(tiles):
+                flipped = words_psum.tile([P, COMPONENTS, P], F32, name="flipped", tag="words")
                 for c in range(COMPONENTS):
                     nc.tensor.transpose(
                         out=flipped[:, c, :],
-                        in_=x_words[:, c * WORDS : (c + 1) * WORDS],
+                        in_=rows[:, FIRST_TILE[s] + t, c * WORDS : (c + 1) * WORDS],
                         identity=identity[:],
                     )
                 nc.scalar.copy(
@@ -155,29 +152,28 @@ def tile_quaternionlinear_t_kernel(tc, x, Wr, Wi, Wj, Wk, br, bi, bj, bk, out):
                 )
 
         def quantise_group(s):
-            x_codes[s] = mx_pool.tile([P, TILES, PASSES, P], U32, name="x_codes", align_bytes=64)
-            x_scales[s] = mx_pool.tile([P, TILES, PASSES, P], U8, name="x_scales", align_bytes=64)
-            nc.vector.quantize_mx(
-                out=x_codes[s][:].rearrange("p t g r -> p (t g r)").bitcast(FP8X4),
-                scales=x_scales[s][:].rearrange("p t g r -> p (t g r)"),
-                in_=x_grouped[s][:],
-            )
+            tiles = GROUPS[s]
+            x_codes[s] = mx_pool.tile([P, tiles, PASSES, P], U32, name="x_codes", align_bytes=64)
+            x_scales[s] = mx_pool.tile([P, tiles, PASSES, P], U8, name="x_scales", align_bytes=64)
+            codes = x_codes[s][:].rearrange("p t g r -> p (t g r)")
+            scales = x_scales[s][:].rearrange("p t g r -> p (t g r)")
+            for first in range(0, tiles, TILES_OF_A_QUANTIZE):
+                end = min(first + TILES_OF_A_QUANTIZE, tiles)
+                words = slice(first * PASSES * P, end * PASSES * P)
+                nc.vector.quantize_mx(
+                    out=codes[:, words].bitcast(FP8X4),
+                    scales=scales[:, words],
+                    in_=x_grouped[s][:, words.start * PACK : words.stop * PACK],
+                )
 
         def multiply_group(s):
-            b, first_tile = s // BLOCK_GROUPS, (s % BLOCK_GROUPS) * TILES
-            if first_tile == 0:
-                out_blocks[b] = out_pool.tile([P, BLOCK_TILES, N_OUT], F32, name="out_block")
-            out_view = out[b * BLOCK_ROWS : (b + 1) * BLOCK_ROWS, :].rearrange(
-                "(p j) n -> p j n", j=BLOCK_TILES
-            )
-            piece = EDGE_TILES if b == BLOCKS - 1 else BLOCK_TILES
-            for t in range(TILES):
-                j = first_tile + t
-                acc = acc_psum.tile([P, N_OUT], F32, name="acc", tag="acc")
+            for t in range(GROUPS[s]):
+                j = FIRST_TILE[s] + t
+                accs[j] = acc_psum.tile([P, N_OUT], F32, name="acc")
                 for g in range(PASSES):
                     strip_cols = slice((1 - g) * PART_COLS, (1 - g) * PART_COLS + N_OUT)
                     nc.tensor.matmul_mx(
-                        out=acc[:],
+                        out=accs[j][:],
                         lhsT=x_codes[s][:, t, g, :].bitcast(FP8X4),
                         lhsT_scale=x_scales[s][:, t, g, :],
                         rhs=w_codes[:, strip_cols].bitcast(FP8X4),
@@ -185,16 +181,18 @@ def tile_quaternionlinear_t_kernel(tc, x, Wr, Wi, Wj, Wk, br, bi, bj, bk, out):
                         start=(g == 0),
                         stop=(g == PASSES - 1),
                     )
-                nc.vector.tensor_add(out=out_blocks[b][:, j, :], in0=acc[:], in1=bias[:])
-                if (j + 1) % piece == 0:
-                    done = slice(j + 1 - piece, j + 1)
-                    nc.sync.dma_start(out=out_view[:, done, :], in_=out_blocks[b][:, done, :])
+                nc.vector.tensor_add(out=rows[:, j, :], in0=accs[j][:], in1=bias[:])
+                if j + 1 in stores:
+                    done = slice(j + 1 - stores[j + 1], j + 1)
+                    nc.sync.dma_start(out=out_view[:, done, :], in_=rows[:, done, :])
+
+        stores = {sum(STORES[: i + 1]): n for i, n in enumerate(STORES)}
 
         for s in range(2):
             transpose_group(s)
             quantise_group(s)
 
-        bias_psum = acc_psum.tile([P, N_OUT], F32, name="bias_psum", tag="acc")
+        bias_psum = words_psum.tile([P, N_OUT], F32, name="bias_psum", tag="words")
         for o in range(COMPONENTS):
             nc.tensor.matmul(
                 out=bias_psum[:, o * QUARTER_OUT : (o + 1) * QUARTER_OUT],
@@ -207,10 +205,10 @@ def tile_quaternionlinear_t_kernel(tc, x, Wr, Wi, Wj, Wk, br, bi, bj, bk, out):
         nc.scalar.copy(out=bias[:], in_=bias_psum[:])
 
         transposed = 2
-        for s in range(GROUPS):
+        for s in range(len(GROUPS)):
             multiply_group(s)
-            while transposed < min(s + 1 + TRANSPOSED_AHEAD, GROUPS):
+            while transposed < min(s + 1 + TRANSPOSED_AHEAD, len(GROUPS)):
                 transpose_group(transposed)
                 transposed += 1
-            if s + 2 < GROUPS:
+            if s + 2 < len(GROUPS):
                 quantise_group(s + 2)

@@ -15,15 +15,14 @@ COMPONENTS = 4
 QUARTER_OUT = N_OUT // COMPONENTS
 WORDS = K_IN // COMPONENTS // 2
 PASSES = 2
-TILES_OF_A_QUANTIZE = 4
 PACK = 4
 ROW_TILES = ROWS // P
-LOADS = (2, 2, 4, 4, 4, 4, 4, 8, 8, 8, 8, 8)
+LOADS = (2, 2, 4, 4, 4, 8, 8, 16, 16)
 LOADS_BEFORE_BIAS = 2
-STORES = (8,) * 7 + (2,) * 4
-GROUPS = (2, 2, 2, 2, 4, 4) + (6,) * 8
+STORES = (8, 8, 16, 8, 8, 8, 4, 2, 2)
+GROUPS = (2,) * 4 + (4,) * 12 + (2,) * 4
 FIRST_TILE = [sum(GROUPS[:s]) for s in range(len(GROUPS))]
-WORDS_BANKS, ACC_BANKS = 5, 3
+WORDS_BANKS, ACC_BANKS = 4, 4
 TRANSPOSED_AHEAD = 3
 
 FLOPS = 2 * ROWS * K_IN * N_OUT
@@ -155,16 +154,11 @@ def tile_quaternionlinear_t_kernel(tc, x, Wr, Wi, Wj, Wk, br, bi, bj, bk, out):
             tiles = GROUPS[s]
             x_codes[s] = mx_pool.tile([P, tiles, PASSES, P], U32, name="x_codes", align_bytes=64)
             x_scales[s] = mx_pool.tile([P, tiles, PASSES, P], U8, name="x_scales", align_bytes=64)
-            codes = x_codes[s][:].rearrange("p t g r -> p (t g r)")
-            scales = x_scales[s][:].rearrange("p t g r -> p (t g r)")
-            for first in range(0, tiles, TILES_OF_A_QUANTIZE):
-                end = min(first + TILES_OF_A_QUANTIZE, tiles)
-                words = slice(first * PASSES * P, end * PASSES * P)
-                nc.vector.quantize_mx(
-                    out=codes[:, words].bitcast(FP8X4),
-                    scales=scales[:, words],
-                    in_=x_grouped[s][:, words.start * PACK : words.stop * PACK],
-                )
+            nc.vector.quantize_mx(
+                out=x_codes[s][:].rearrange("p t g r -> p (t g r)").bitcast(FP8X4),
+                scales=x_scales[s][:].rearrange("p t g r -> p (t g r)"),
+                in_=x_grouped[s][:],
+            )
 
         def multiply_group(s):
             for t in range(GROUPS[s]):

from contextlib import ExitStack

import concourse.mybir as mybir
from concourse.masks import make_identity

BF16 = mybir.dt.bfloat16
F32 = mybir.dt.float32
U32 = mybir.dt.uint32
U8 = mybir.dt.uint8
FP8X4 = mybir.dt.float8_e4m3fn_x4

P = 128
ROWS, K_IN, N_OUT = 8192, 1024, 512
COMPONENTS = 4
QUARTER_OUT = N_OUT // COMPONENTS
WORDS = K_IN // COMPONENTS // 2
PASSES = 2
PACK = 4
ROW_TILES = ROWS // P
LOADS = (2, 2, 4, 4, 4, 8, 8, 16, 16)
LOADS_BEFORE_BIAS = 2
STORES = (8, 8, 16, 8, 8, 8, 4, 2, 2)
GROUPS = (2,) * 4 + (4,) * 12 + (2,) * 4
FIRST_TILE = [sum(GROUPS[:s]) for s in range(len(GROUPS))]
WORDS_BANKS, ACC_BANKS = 4, 4
TRANSPOSED_AHEAD = 3

FLOPS = 2 * ROWS * K_IN * N_OUT

SLOTS = ("+i", "+r", "-i", "-k", "+j", "+k", "-j", "-k again")
STRIP = (
    (("-j", "-k again"), ("-k", "+j")),
    (("+r", "-i"), ("+i", "+r")),
    (("+j", "+k"), ("+k", "-j")),
)
PART_COLS = 2 * QUARTER_OUT
STRIP_COLS = len(STRIP) * PART_COLS

BIAS_SIGNS = (
    (1.0, -1.0, -1.0, -1.0),
    (1.0, 1.0, 1.0, -1.0),
    (1.0, -1.0, 1.0, 1.0),
    (1.0, 1.0, -1.0, 1.0),
)
QUADRANT = 32


def tile_quaternionlinear_t_kernel(tc, x, Wr, Wi, Wj, Wk, br, bi, bj, bk, out):
    nc = tc.nc
    with ExitStack() as stack:
        consts = stack.enter_context(tc.tile_pool(name="consts", bufs=1))
        rows_pool = stack.enter_context(tc.tile_pool(name="rows_pool", bufs=1))
        mx_pool = stack.enter_context(tc.tile_pool(name="mx_pool", bufs=2))
        words_psum = stack.enter_context(tc.psum_pool(name="words_psum", bufs=WORDS_BANKS))
        acc_psum = stack.enter_context(tc.psum_pool(name="acc_psum", bufs=ACC_BANKS))
        stack.enter_context(tc.manual_schedule())

        rows = rows_pool.tile([P, ROW_TILES, N_OUT], F32, name="rows", align_bytes=64)
        x_view = x.rearrange("(p j) k -> p j k", j=ROW_TILES)
        out_view = out.rearrange("(p j) n -> p j n", j=ROW_TILES)

        def load_rows(first, tiles):
            nc.sync.dma_start(
                out=rows[:, first : first + tiles, :].bitcast(BF16),
                in_=x_view[:, first : first + tiles, :],
            )

        x_loads = [(n, sum(LOADS[:i])) for i, n in enumerate(LOADS)]

        w_slots = consts.tile([P, len(SLOTS), 2, QUARTER_OUT], BF16, name="w_slots")
        for slot, w in ((0, Wi), (1, Wr), (4, Wj), (5, Wk)):
            nc.sync.dma_start(
                out=w_slots[:, slot, :, :], in_=w.rearrange("(p e) n -> p e n", e=2)
            )
        for tiles, first in x_loads[:LOADS_BEFORE_BIAS]:
            load_rows(first, tiles)
        bias_rows = consts.tile([P, QUARTER_OUT], BF16, name="bias_rows")
        nc.vector.memset(bias_rows[:], 0.0)
        for m, bias_vector in enumerate((br, bi, bj, bk)):
            nc.sync.dma_start(
                out=bias_rows[m * QUADRANT : m * QUADRANT + 1, :],
                in_=bias_vector.rearrange("(o n) -> o n", o=1),
            )
        for tiles, first in x_loads[LOADS_BEFORE_BIAS:]:
            load_rows(first, tiles)

        identity = consts.tile([P, P], F32, name="identity")
        make_identity(nc, identity[:])

        bias_signs = consts.tile([P, COMPONENTS, P], BF16, name="bias_signs")
        nc.vector.memset(bias_signs[:], 1.0)
        for o in range(COMPONENTS):
            for m in range(COMPONENTS):
                if BIAS_SIGNS[o][m] < 0.0:
                    nc.vector.memset(bias_signs[m * QUADRANT : (m + 1) * QUADRANT, o, :], -1.0)

        w_grouped = consts.tile([P, STRIP_COLS, PACK], BF16, name="w_grouped", align_bytes=64)
        w_codes = consts.tile([P, STRIP_COLS], U32, name="w_codes", align_bytes=64)
        w_scales = consts.tile([P, STRIP_COLS], U8, name="w_scales", align_bytes=64)
        nc.vector.tensor_scalar_mul(
            out=w_slots[:, 2:4, :, :], in0=w_slots[:, 0:6:5, :, :], scalar1=-1.0
        )
        nc.vector.tensor_scalar_mul(
            out=w_slots[:, 6:8, :, :], in0=w_slots[:, 4:6, :, :], scalar1=-1.0
        )
        for part, half in ((1, 0), (1, 1), (2, 0), (2, 1), (0, 0), (0, 1)):
            upper, lower = STRIP[part][half]
            slot = SLOTS.index(upper)
            assert SLOTS[slot + 1] == lower
            first_col = part * PART_COLS + half * QUARTER_OUT
            copy = nc.scalar.copy if part == 0 else nc.vector.tensor_copy
            copy(
                out=w_grouped[:, first_col : first_col + QUARTER_OUT, :].rearrange(
                    "p n (u e) -> p n u e", u=2
                ),
                in_=w_slots[:, slot : slot + 2, :, :].rearrange("p u e n -> p n u e"),
            )
        for cols in (slice(PART_COLS, STRIP_COLS), slice(0, PART_COLS)):
            nc.vector.quantize_mx(
                out=w_codes[:, cols].bitcast(FP8X4),
                scales=w_scales[:, cols],
                in_=w_grouped[:, cols, :].rearrange("p n t -> p (n t)"),
            )

        x_grouped = {}
        x_codes = {}
        x_scales = {}
        accs = {}

        def transpose_group(s):
            tiles = GROUPS[s]
            x_grouped[s] = mx_pool.tile(
                [P, tiles * PASSES * P * PACK], BF16, name="x_grouped", align_bytes=64
            )
            grouped_words = (
                x_grouped[s][:]
                .bitcast(F32)
                .rearrange("p (t g r u) -> p t g r u", t=tiles, g=PASSES, r=P)
            )
            for t in range(tiles):
                flipped = words_psum.tile([P, COMPONENTS, P], F32, name="flipped", tag="words")
                for c in range(COMPONENTS):
                    nc.tensor.transpose(
                        out=flipped[:, c, :],
                        in_=rows[:, FIRST_TILE[s] + t, c * WORDS : (c + 1) * WORDS],
                        identity=identity[:],
                    )
                nc.scalar.copy(
                    out=grouped_words[:, t, :, :, :],
                    in_=flipped[:].rearrange("p (g u) r -> p g r u", u=2),
                )

        def quantise_group(s):
            tiles = GROUPS[s]
            x_codes[s] = mx_pool.tile([P, tiles, PASSES, P], U32, name="x_codes", align_bytes=64)
            x_scales[s] = mx_pool.tile([P, tiles, PASSES, P], U8, name="x_scales", align_bytes=64)
            nc.vector.quantize_mx(
                out=x_codes[s][:].rearrange("p t g r -> p (t g r)").bitcast(FP8X4),
                scales=x_scales[s][:].rearrange("p t g r -> p (t g r)"),
                in_=x_grouped[s][:],
            )

        def multiply_group(s):
            for t in range(GROUPS[s]):
                j = FIRST_TILE[s] + t
                accs[j] = acc_psum.tile([P, N_OUT], F32, name="acc")
                for g in range(PASSES):
                    strip_cols = slice((1 - g) * PART_COLS, (1 - g) * PART_COLS + N_OUT)
                    nc.tensor.matmul_mx(
                        out=accs[j][:],
                        lhsT=x_codes[s][:, t, g, :].bitcast(FP8X4),
                        lhsT_scale=x_scales[s][:, t, g, :],
                        rhs=w_codes[:, strip_cols].bitcast(FP8X4),
                        rhs_scale=w_scales[:, strip_cols],
                        start=(g == 0),
                        stop=(g == PASSES - 1),
                    )
                nc.vector.tensor_add(out=rows[:, j, :], in0=accs[j][:], in1=bias[:])
                if j + 1 in stores:
                    done = slice(j + 1 - stores[j + 1], j + 1)
                    nc.sync.dma_start(out=out_view[:, done, :], in_=rows[:, done, :])

        stores = {sum(STORES[: i + 1]): n for i, n in enumerate(STORES)}

        for s in range(2):
            transpose_group(s)
            quantise_group(s)

        bias_psum = words_psum.tile([P, N_OUT], F32, name="bias_psum", tag="words")
        for o in range(COMPONENTS):
            nc.tensor.matmul(
                out=bias_psum[:, o * QUARTER_OUT : (o + 1) * QUARTER_OUT],
                lhsT=bias_signs[:, o, :],
                rhs=bias_rows[:],
                start=True,
                stop=True,
            )
        bias = consts.tile([P, N_OUT], F32, name="bias")
        nc.scalar.copy(out=bias[:], in_=bias_psum[:])

        transposed = 2
        for s in range(len(GROUPS)):
            multiply_group(s)
            while transposed < min(s + 1 + TRANSPOSED_AHEAD, len(GROUPS)):
                transpose_group(transposed)
                transposed += 1
            if s + 2 < len(GROUPS):
                quantise_group(s + 2)
